import numpy as np
import ml_dtypes


def mxq(x, axis, fmt="e4m3"):
    dtype, down = {"e4m3": (ml_dtypes.float8_e4m3fn, 7), "e5m2": (ml_dtypes.float8_e5m2, 14)}[fmt]
    v = np.moveaxis(np.asarray(x, np.float32).astype(ml_dtypes.bfloat16).astype(np.float64), axis, -1)
    blocks = v.reshape(v.shape[:-1] + (-1, 32))
    amax = np.abs(blocks).max(-1, keepdims=True)
    byte = np.maximum(np.where(amax > 0, np.frexp(amax)[1] - 1 + 127, 0) - down, 1)
    scale = np.exp2(byte - 127.0)
    codes = (blocks / scale).astype(np.float32).astype(dtype).astype(np.float64)
    return np.moveaxis((codes * scale).reshape(v.shape), -1, axis)


WIDE = False


def mx_kscale(k):
    if not WIDE:
        return np.ones(k)
    levels = np.array([10, -10, 5, -5, 0])
    if k % 512:
        return np.exp2(np.random.permutation(np.resize(levels, k // 32))).repeat(32)
    a = np.empty((k // 512, 16))
    for p in range(k // 512):
        a[p, :8] = np.random.permutation(np.resize(levels, 8))
        for g in range(8):
            far = levels[np.abs(levels - a[p, g]) >= 10]
            a[p, g + 8] = far[np.random.randint(len(far))]
    return np.exp2(a.ravel()).repeat(32)


BF16 = ml_dtypes.bfloat16


def bf(x):
    return np.asarray(x, np.float32).astype(BF16)


def f64(x):
    return np.asarray(x).astype(np.float64)


B, S, E, H = 4, 256, 1024, 16
DH = E // H
EPS = 1e-5


def heads(t):
    return t.reshape(B, S, H, DH).transpose(0, 2, 1, 3)


def setup_inputs():
    s = mx_kscale(E)
    tok = np.exp2(np.random.uniform(-7.5, 1.5, (B, S, 1)))
    off = 0.5 * np.random.standard_normal((B, S, 1))
    return {"inputs": bf((np.random.standard_normal((B, S, E)) + off) * tok),
            "ln_w": bf((1.0 + 0.1 * np.random.standard_normal(E)) * s),
            "ln_b": bf(0.1 * np.random.standard_normal(E) * s),
            "w_qkv": bf(np.random.standard_normal((3 * E, E)) / np.sqrt(E) / s[None, :])}


def reference(inputs, ln_w, ln_b, w_qkv):
    a = f64(inputs)
    mu = a.mean(-1, keepdims=True)
    var = a.var(-1, keepdims=True)
    x = (a - mu) / np.sqrt(var + EPS) * f64(ln_w) + f64(ln_b)
    qkv = mxq(x, 2, "e4m3") @ mxq(f64(w_qkv), 1, "e4m3").T
    q, k, v = np.split(qkv, 3, axis=-1)
    return heads(q), heads(k), heads(v)

@@ -1,0 +1,240 @@
+from contextlib import ExitStack
+
+import concourse.mybir as mybir
+from concourse.masks import make_identity
+
+FLOPS = 2 * 1024 * 3072 * 1024
+
+F32 = mybir.dt.float32
+BF16 = mybir.dt.bfloat16
+U32 = mybir.dt.uint32
+U8 = mybir.dt.uint8
+FP8X4 = mybir.dt.float8_e4m3fn_x4
+ALU = mybir.AluOpType
+ACT = mybir.ActivationFunctionType
+
+P = 128
+B = 4
+E = 1024
+EPS = 1e-5
+TILES = 8
+CHUNKS = 6
+
+
+def tile_selfattention_pa_kernel(tc, inputs, ln_w, ln_b, w_qkv, out_0, out_1, out_2):
+    nc = tc.nc
+    outs = (out_0, out_1, out_2)
+    with ExitStack() as ctx:
+        const = ctx.enter_context(tc.tile_pool(name="const", bufs=1))
+        wraw_pool = ctx.enter_context(tc.tile_pool(name="wraw", bufs=CHUNKS))
+        gw_pool = ctx.enter_context(tc.tile_pool(name="gw", bufs=2))
+        xh_pool = ctx.enter_context(tc.tile_pool(name="xh", bufs=8))
+        pl_pool = ctx.enter_context(tc.tile_pool(name="pl", bufs=2))
+        gx_pool = ctx.enter_context(tc.tile_pool(name="gx", bufs=2))
+        o_pool = ctx.enter_context(tc.tile_pool(name="o", bufs=6))
+        ps_pool = ctx.enter_context(tc.psum_pool(name="ps", bufs=8))
+        ctx.enter_context(tc.manual_schedule())
+
+        ident = const.tile([P, P], F32)
+        one = const.tile([P, 1], F32)
+        warm = const.tile([P, 1], F32)
+        lnrow = const.tile([P, 512], BF16)
+        lnf = const.tile([P, 4, P], F32)
+        wb = const.tile([P, 4, 4], F32)
+        x_sb = {}
+        xc = const.tile([P, 2 * 2 * 512], U32, align_bytes=64)
+        xs = const.tile([P, 2 * 2 * 512], U8, align_bytes=64)
+        wc = const.tile([P, CHUNKS * 1024], U32, align_bytes=64)
+        ws = const.tile([P, CHUNKS * 1024], U8, align_bytes=64)
+        st = const.tile([P, TILES, 2, 6], F32)
+        mv = const.tile([P, TILES, 2], F32)
+        std = const.tile([P, TILES], F32)
+        rstd = const.tile([P, TILES], F32)
+        negmu = const.tile([P, TILES], F32)
+        wraw = []
+        xh = {}
+
+        def copy_on(eng, dst, src):
+            if eng == "v":
+                nc.vector.tensor_copy(out=dst, in_=src)
+            else:
+                nc.scalar.copy(out=dst, in_=src)
+
+        def bank():
+            return ps_pool.tile([P, 4, P], F32, name="bank", tag="ps")
+
+        def load_x(j0, j1):
+            x_t = const.tile([P, j1 - j0, E], BF16, name="x_t%d" % j0)
+            for b in range(B):
+                nc.sync.dma_start(
+                    out=x_t[b:P:4, :, :],
+                    in_=inputs[b].rearrange("(pp j) k -> pp j k", j=TILES)[:, j0:j1, :],
+                )
+            for j in range(j0, j1):
+                x_sb[j] = x_t[:, j - j0, :]
+
+        def load_w(c):
+            w_t = wraw_pool.tile([P, 4 * E], BF16, name="wraw_t", tag="wraw")
+            nc.sync.dma_start(
+                out=w_t[:].rearrange("p (r k) -> p r k", r=4),
+                in_=w_qkv[512 * c : 512 * c + 512, :].rearrange("(r p) k -> p r k", p=P),
+            )
+            wraw.append(w_t)
+
+        def statistics(j):
+            for h in range(2):
+                nc.vector.bn_stats(out=st[:, j, h, :], in_=x_sb[j][:, 512 * h : 512 * h + 512])
+            nc.vector.bn_aggr(out=mv[:, j, :], in_=st[:, j, :, :].rearrange("p a b -> p (a b)"))
+            nc.scalar.activation(out=std[:, j : j + 1], in_=mv[:, j, 1:2], func=ACT.Sqrt, bias=EPS)
+
+        def normalise(j):
+            nc.vector.reciprocal(out=rstd[:, j : j + 1], in_=std[:, j : j + 1])
+            nc.vector.tensor_scalar_mul(out=negmu[:, j : j + 1], in0=mv[:, j, 0:1], scalar1=-1.0)
+            t = xh_pool.tile([P, 8, P], F32, name="xh_t", tag="xh")
+            nc.gpsimd.tensor_scalar(
+                out=t[:].rearrange("p (g t) q -> p g t q", t=4),
+                in0=x_sb[j].rearrange("p (g q t) -> p g t q", g=2, t=4),
+                scalar1=negmu[:, j : j + 1],
+                scalar2=rstd[:, j : j + 1],
+                op0=ALU.add,
+                op1=ALU.mult,
+            )
+            xh[j] = t
+
+        gw = {}
+
+        def w_transposes(c, r):
+            t = bank()
+            wf = wraw[c][:].bitcast(F32)
+            for gu in range(4):
+                first = 512 * r + 256 * (gu // 2) + gu % 2
+                nc.tensor.transpose(t[:, gu, :], wf[:, first : first + 255 : 2], ident[:])
+            return t
+
+        def w_copy(c, r, t, eng):
+            if c not in gw:
+                gw[c] = gw_pool.tile([P, 4096], BF16, name="gw_t", tag="gw", align_bytes=64)
+            gwf = gw[c][:].bitcast(F32).rearrange("p (g n u) -> p g n u", g=2, u=2)
+            copy_on(eng, gwf[:, :, P * r : P * r + P, :], t[:].rearrange("p (g u) f -> p g f u", u=2))
+
+        def w_quantise(c):
+            sl = slice(c * 1024, c * 1024 + 1024)
+            nc.vector.quantize_mx(out=wc[:, sl].bitcast(FP8X4), scales=ws[:, sl], in_=gw[c][:])
+
+        def prepare_w(c, engines):
+            banks = [w_transposes(c, r) for r in range(4)]
+            for r in range(4):
+                w_copy(c, r, banks[r], engines[r])
+            w_quantise(c)
+
+        def x_regroup(planes):
+            gx = gx_pool.tile([P, 512, 4], BF16, name="gx_t", tag="gx", align_bytes=64)
+            nc.vector.tensor_copy(
+                out=gx[:].rearrange("p (c i) t -> p c t i", i=4),
+                in_=planes[:].rearrange("p t (c i) -> p c t i", i=4),
+            )
+            return gx
+
+        def x_quantise(q, g, gx):
+            sl = slice((2 * q + g) * 512, (2 * q + g) * 512 + 512)
+            nc.vector.quantize_mx(out=xc[:, sl].bitcast(FP8X4), scales=xs[:, sl], in_=gx[:].rearrange("p n t -> p (n t)"))
+
+        def prepare_x(q, between):
+            planes = [pl_pool.tile([P, 4, 512], BF16, name="planes", tag="pl") for g in range(2)]
+            gx = [None, None]
+            for t in range(8):
+                g, t4 = t // 4, t % 4
+                xt = bank()
+                for jq in range(4):
+                    nc.tensor.transpose(xt[:, jq, :], xh[4 * q + jq][:, t, :], ident[:])
+                src = xt[:].rearrange("p a b -> p (a b)")
+                if t % 2 == 1:
+                    nc.vector.tensor_scalar(
+                        out=planes[g][:, t4, :], in0=src,
+                        scalar1=wb[:, t4, g : g + 1], scalar2=wb[:, t4, 2 + g : 3 + g],
+                        op0=ALU.mult, op1=ALU.add,
+                    )
+                else:
+                    nc.scalar.activation(
+                        out=planes[g][:, t4, :], in_=src, func=ACT.Identity,
+                        scale=wb[:, t4, g : g + 1], bias=wb[:, t4, 2 + g : 3 + g],
+                    )
+                if t == 3 and between is not None:
+                    between()
+                if t == 5:
+                    gx[0] = x_regroup(planes[0])
+            gx[1] = x_regroup(planes[1])
+            x_quantise(q, 0, gx[0])
+            x_quantise(q, 1, gx[1])
+
+        def project(c, q, engines):
+            accs = []
+            for jq in range(4):
+                acc = bank()
+                for g in range(2):
+                    xo = (2 * q + g) * 512 + P * jq
+                    wo = c * 1024 + 512 * g
+                    nc.tensor.matmul_mx(
+                        out=acc[:].rearrange("p a b -> p (a b)"),
+                        lhsT=xc[:, xo : xo + P].bitcast(FP8X4), lhsT_scale=xs[:, xo : xo + P],
+                        rhs=wc[:, wo : wo + 512].bitcast(FP8X4), rhs_scale=ws[:, wo : wo + 512],
+                        start=(g == 0), stop=(g == 1),
+                    )
+                accs.append(acc)
+            o_t = o_pool.tile([P, 8, 4, 64], F32, name="o_t", tag="o")
+            for jq in range(4):
+                copy_on(engines[jq], o_t[:, :, jq, :], accs[jq][:].rearrange("p a (x d) -> p (a x) d", d=64))
+            h0 = 8 * (c % 2)
+            for b in range(B):
+                nc.sync.dma_start(
+                    out=outs[c // 2][b, h0 : h0 + 8, :, :].rearrange("h (pp j) d -> pp h j d", j=TILES)[:, :, 4 * q : 4 * q + 4, :],
+                    in_=o_t[b:P:4, :, :, :],
+                )
+
+        nc.vector.memset(lnrow[:], 0.0)
+        nc.scalar.dma_start(out=lnrow[0:2, :], in_=ln_w.rearrange("(r c) -> r c", c=512))
+        nc.scalar.dma_start(out=lnrow[2:4, :], in_=ln_b.rearrange("(r c) -> r c", c=512))
+        load_x(0, 1)
+        load_x(1, 2)
+        load_x(2, 4)
+        load_w(0)
+        load_x(4, 8)
+        for c in range(1, CHUNKS):
+            load_w(c)
+        make_identity(nc, ident[:])
+        nc.vector.memset(one[:], 1.0)
+        nc.scalar.activation(out=warm[:], in_=one[:], func=ACT.Sqrt)
+
+        for k in range(TILES + 1):
+            if k < TILES:
+                statistics(k)
+            if k >= 1:
+                normalise(k - 1)
+            if k == 1:
+                nc.vector.tensor_copy(out=lnf[:], in_=lnrow[:].rearrange("p (q e) -> p e q", e=4))
+                lnt = bank()
+                for e in range(4):
+                    nc.tensor.transpose(lnt[:, e, :], lnf[:, e, :], ident[:])
+            if k == 2:
+                nc.vector.tensor_copy(out=wb[:], in_=lnt[:, :, 0:4])
+            if k in (3, 4):
+                for r in (2 * (k - 3), 2 * (k - 3) + 1):
+                    w_copy(0, r, w_transposes(0, r), "s")
+
+        prepare_x(0, lambda: w_quantise(0))
+        prepare_w(1, "ssss")
+        prepare_w(2, "ssss")
+        project(0, 0, "sssv")
+        prepare_x(1, None)
+        project(1, 0, "sssv")
+        project(2, 0, "sssv")
+        project(0, 1, "svsv")
+        project(1, 1, "svsv")
+        prepare_w(3, "svsv")
+        project(2, 1, "svsv")
+        prepare_w(4, "svsv")
+        for c in range(3, CHUNKS):
+            project(c, 0, "svsv")
+            if c == 3:
+                prepare_w(5, "svsv")
+            project(c, 1, "svsv")

@@ -18,7 +18,10 @@ B = 4
 E = 1024
 EPS = 1e-5
 TILES = 8
-CHUNKS = 6
+CHUNKS = 12
+W_BUFS = 8
+SCALAR_TILES = (1,)
+REORDERED = range(6, CHUNKS)
 
 
 def tile_selfattention_pa_kernel(tc, inputs, ln_w, ln_b, w_qkv, out_0, out_1, out_2):
@@ -26,33 +29,35 @@ def tile_selfattention_pa_kernel(tc, inputs, ln_w, ln_b, w_qkv, out_0, out_1, ou
     outs = (out_0, out_1, out_2)
     with ExitStack() as ctx:
         const = ctx.enter_context(tc.tile_pool(name="const", bufs=1))
-        wraw_pool = ctx.enter_context(tc.tile_pool(name="wraw", bufs=CHUNKS))
-        gw_pool = ctx.enter_context(tc.tile_pool(name="gw", bufs=2))
+        wraw_pool = ctx.enter_context(tc.tile_pool(name="wraw", bufs=W_BUFS))
+        wp_pool = ctx.enter_context(tc.tile_pool(name="wp", bufs=2))
+        gw_pool = ctx.enter_context(tc.tile_pool(name="gw", bufs=6))
         xh_pool = ctx.enter_context(tc.tile_pool(name="xh", bufs=8))
-        pl_pool = ctx.enter_context(tc.tile_pool(name="pl", bufs=2))
+        pl_pool = ctx.enter_context(tc.tile_pool(name="pl", bufs=4))
         gx_pool = ctx.enter_context(tc.tile_pool(name="gx", bufs=2))
         o_pool = ctx.enter_context(tc.tile_pool(name="o", bufs=6))
         ps_pool = ctx.enter_context(tc.psum_pool(name="ps", bufs=8))
         ctx.enter_context(tc.manual_schedule())
 
         ident = const.tile([P, P], F32)
+        perm = const.tile([P, P], F32)
         one = const.tile([P, 1], F32)
         warm = const.tile([P, 1], F32)
         lnrow = const.tile([P, 512], BF16)
         lnf = const.tile([P, 4, P], F32)
         wb = const.tile([P, 4, 4], F32)
-        x_sb = {}
         xc = const.tile([P, 2 * 2 * 512], U32, align_bytes=64)
         xs = const.tile([P, 2 * 2 * 512], U8, align_bytes=64)
-        wc = const.tile([P, CHUNKS * 1024], U32, align_bytes=64)
-        ws = const.tile([P, CHUNKS * 1024], U8, align_bytes=64)
+        wc = const.tile([P, CHUNKS * 512], U32, align_bytes=64)
+        ws = const.tile([P, CHUNKS * 512], U8, align_bytes=64)
         st = const.tile([P, TILES, 2, 6], F32)
         mv = const.tile([P, TILES, 2], F32)
-        std = const.tile([P, TILES], F32)
         rstd = const.tile([P, TILES], F32)
         negmu = const.tile([P, TILES], F32)
-        wraw = []
-        xh = {}
+        junk = const.tile([P, E], BF16)
+        sums = const.tile([P, TILES, 2], F32)
+        x_sb, xh, wraw, gw, wp, o_sb, planes, gx = {}, {}, {}, {}, {}, {}, {}, {}
+        w_bank, x_bank, p_bank, ln_bank = {}, {}, {}, {}
 
         def copy_on(eng, dst, src):
             if eng == "v":
@@ -63,178 +68,270 @@ def tile_selfattention_pa_kernel(tc, inputs, ln_w, ln_b, w_qkv, out_0, out_1, ou
         def bank():
             return ps_pool.tile([P, 4, P], F32, name="bank", tag="ps")
 
+        x_rows = inputs.flatten_outer_dims().rearrange("(p j) k -> p j k", j=TILES)
+
         def load_x(j0, j1):
             x_t = const.tile([P, j1 - j0, E], BF16, name="x_t%d" % j0)
-            for b in range(B):
-                nc.sync.dma_start(
-                    out=x_t[b:P:4, :, :],
-                    in_=inputs[b].rearrange("(pp j) k -> pp j k", j=TILES)[:, j0:j1, :],
-                )
+            nc.sync.dma_start(out=x_t[:], in_=x_rows[:, j0:j1, :])
             for j in range(j0, j1):
                 x_sb[j] = x_t[:, j - j0, :]
 
+        def load_ln():
+            nc.sync.dma_start(out=lnrow[0:2, :], in_=ln_w.rearrange("(r c) -> r c", c=512))
+            nc.sync.dma_start(out=lnrow[2:4, :], in_=ln_b.rearrange("(r c) -> r c", c=512))
+
         def load_w(c):
-            w_t = wraw_pool.tile([P, 4 * E], BF16, name="wraw_t", tag="wraw")
+            w_t = wraw_pool.tile([P, 2 * E], BF16, name="wraw_t", tag="wraw")
             nc.sync.dma_start(
-                out=w_t[:].rearrange("p (r k) -> p r k", r=4),
-                in_=w_qkv[512 * c : 512 * c + 512, :].rearrange("(r p) k -> p r k", p=P),
+                out=w_t[:].rearrange("p (r k) -> p r k", r=2),
+                in_=w_qkv[256 * c : 256 * c + 256, :].rearrange("(r p) k -> p r k", p=P),
             )
-            wraw.append(w_t)
+            wraw[c] = w_t
 
         def statistics(j):
+            if j in SCALAR_TILES:
+                nc.scalar.activation(out=junk[:], in_=x_sb[j], func=ACT.Identity, accum_out=sums[:, j, 0:1])
+                nc.scalar.activation(out=negmu[:, j : j + 1], in_=sums[:, j, 0:1], func=ACT.Identity, scale=-1.0 / E)
+                nc.scalar.activation(
+                    out=junk[:], in_=x_sb[j], func=ACT.Square, bias=negmu[:, j : j + 1], accum_out=sums[:, j, 1:2]
+                )
+                return
             for h in range(2):
                 nc.vector.bn_stats(out=st[:, j, h, :], in_=x_sb[j][:, 512 * h : 512 * h + 512])
             nc.vector.bn_aggr(out=mv[:, j, :], in_=st[:, j, :, :].rearrange("p a b -> p (a b)"))
-            nc.scalar.activation(out=std[:, j : j + 1], in_=mv[:, j, 1:2], func=ACT.Sqrt, bias=EPS)
 
-        def normalise(j):
-            nc.vector.reciprocal(out=rstd[:, j : j + 1], in_=std[:, j : j + 1])
-            nc.vector.tensor_scalar_mul(out=negmu[:, j : j + 1], in0=mv[:, j, 0:1], scalar1=-1.0)
-            t = xh_pool.tile([P, 8, P], F32, name="xh_t", tag="xh")
+        def inverse_deviation(j):
+            if j in SCALAR_TILES:
+                nc.scalar.activation(
+                    out=rstd[:, j : j + 1], in_=sums[:, j, 1:2], func=ACT.Abs_reciprocal_sqrt, bias=EPS, scale=1.0 / E
+                )
+            else:
+                nc.scalar.activation(out=rstd[:, j : j + 1], in_=mv[:, j, 1:2], func=ACT.Abs_reciprocal_sqrt, bias=EPS)
+
+        def normalise(j, eng="g"):
+            xh[j] = xh_pool.tile([P, 8, P], F32, name="xh_t", tag="xh")
+            dst = xh[j][:].rearrange("p (g t) q -> p g t q", t=4)
+            src = x_sb[j].rearrange("p (g q t) -> p g t q", g=2, t=4)
+            if eng == "v":
+                nc.vector.tensor_scalar(
+                    out=dst, in0=src, scalar1=mv[:, j, 0:1], scalar2=rstd[:, j : j + 1], op0=ALU.subtract, op1=ALU.mult
+                )
+                return
+            if j not in SCALAR_TILES:
+                nc.gpsimd.tensor_scalar(
+                    out=negmu[:, j : j + 1], in0=mv[:, j, 0:1], scalar1=-1.0, scalar2=0.0, op0=ALU.mult, op1=ALU.add
+                )
             nc.gpsimd.tensor_scalar(
-                out=t[:].rearrange("p (g t) q -> p g t q", t=4),
-                in0=x_sb[j].rearrange("p (g q t) -> p g t q", g=2, t=4),
-                scalar1=negmu[:, j : j + 1],
-                scalar2=rstd[:, j : j + 1],
-                op0=ALU.add,
-                op1=ALU.mult,
+                out=dst, in0=src, scalar1=negmu[:, j : j + 1], scalar2=rstd[:, j : j + 1], op0=ALU.add, op1=ALU.mult
             )
-            xh[j] = t
 
-        gw = {}
+        def layer_norm(j, eng="g"):
+            statistics(j)
+            inverse_deviation(j)
+            normalise(j, eng)
 
-        def w_transposes(c, r):
-            t = bank()
-            wf = wraw[c][:].bitcast(F32)
-            for gu in range(4):
-                first = 512 * r + 256 * (gu // 2) + gu % 2
-                nc.tensor.transpose(t[:, gu, :], wf[:, first : first + 255 : 2], ident[:])
-            return t
+        def ln_rows():
+            nc.scalar.copy(out=lnf[:], in_=lnrow[:].rearrange("p (q e) -> p e q", e=4))
 
-        def w_copy(c, r, t, eng):
+        def ln_transpose():
+            ln_bank[0] = bank()
+            for t in range(4):
+                nc.tensor.transpose(ln_bank[0][:, t, :], lnf[:, t, :], ident[:])
+
+        def ln_evacuate():
+            nc.scalar.copy(out=wb[:], in_=ln_bank[0][:, :, 0:4])
+
+        def w_reorder(c, eng):
+            wp[c] = wp_pool.tile([P, 2 * E], BF16, name="wp_t", tag="wp")
+            for u in range(2):
+                dst = wp[c][:].rearrange("p (rg u q e) -> p u rg q e", rg=4, u=2, e=2)[:, u, :, :, :]
+                src = wraw[c][:].rearrange("p (rg q u e) -> p u rg q e", rg=4, u=2, e=2)[:, u, :, :, :]
+                if eng == "g":
+                    nc.gpsimd.tensor_scalar(out=dst, in0=src, scalar1=1.0, scalar2=0.0, op0=ALU.mult, op1=ALU.add)
+                else:
+                    nc.vector.tensor_copy(out=dst, in_=src)
+
+        def w_transpose(c, g):
+            w_bank[c, g] = bank()
+            words = (wp[c] if c in REORDERED else wraw[c])[:].bitcast(F32)
+            for r in range(2):
+                for u in range(2):
+                    first = 512 * r + 256 * g
+                    if c in REORDERED:
+                        w128 = words[:, first + P * u : first + P * u + P]
+                    else:
+                        w128 = words[:, first + u : first + u + 255 : 2]
+                    nc.tensor.transpose(w_bank[c, g][:, 2 * r + u, :], w128, ident[:])
+            if g == 1 and c + W_BUFS < CHUNKS:
+                load_w(c + W_BUFS)
+
+        def w_evacuate(c, g, eng):
             if c not in gw:
-                gw[c] = gw_pool.tile([P, 4096], BF16, name="gw_t", tag="gw", align_bytes=64)
-            gwf = gw[c][:].bitcast(F32).rearrange("p (g n u) -> p g n u", g=2, u=2)
-            copy_on(eng, gwf[:, :, P * r : P * r + P, :], t[:].rearrange("p (g u) f -> p g f u", u=2))
+                gw[c] = gw_pool.tile([P, 2048], BF16, name="gw_t", tag="gw", align_bytes=64)
+            dst = gw[c][:].bitcast(F32).rearrange("p (g r n u) -> p g r n u", g=2, r=2, u=2)[:, g, :, :, :]
+            copy_on(eng, dst, w_bank[c, g][:].rearrange("p (r u) n -> p r n u", u=2))
+
+        def w_prepare(c, engines):
+            for g in range(2):
+                w_transpose(c, g)
+                w_evacuate(c, g, engines[g])
 
         def w_quantise(c):
-            sl = slice(c * 1024, c * 1024 + 1024)
+            sl = slice(c * 512, c * 512 + 512)
             nc.vector.quantize_mx(out=wc[:, sl].bitcast(FP8X4), scales=ws[:, sl], in_=gw[c][:])
 
-        def prepare_w(c, engines):
-            banks = [w_transposes(c, r) for r in range(4)]
-            for r in range(4):
-                w_copy(c, r, banks[r], engines[r])
-            w_quantise(c)
-
-        def x_regroup(planes):
-            gx = gx_pool.tile([P, 512, 4], BF16, name="gx_t", tag="gx", align_bytes=64)
-            nc.vector.tensor_copy(
-                out=gx[:].rearrange("p (c i) t -> p c t i", i=4),
-                in_=planes[:].rearrange("p t (c i) -> p c t i", i=4),
-            )
-            return gx
-
-        def x_quantise(q, g, gx):
-            sl = slice((2 * q + g) * 512, (2 * q + g) * 512 + 512)
-            nc.vector.quantize_mx(out=xc[:, sl].bitcast(FP8X4), scales=xs[:, sl], in_=gx[:].rearrange("p n t -> p (n t)"))
-
-        def prepare_x(q, between):
-            planes = [pl_pool.tile([P, 4, 512], BF16, name="planes", tag="pl") for g in range(2)]
-            gx = [None, None]
-            for t in range(8):
-                g, t4 = t // 4, t % 4
-                xt = bank()
-                for jq in range(4):
-                    nc.tensor.transpose(xt[:, jq, :], xh[4 * q + jq][:, t, :], ident[:])
-                src = xt[:].rearrange("p a b -> p (a b)")
-                if t % 2 == 1:
-                    nc.vector.tensor_scalar(
-                        out=planes[g][:, t4, :], in0=src,
-                        scalar1=wb[:, t4, g : g + 1], scalar2=wb[:, t4, 2 + g : 3 + g],
-                        op0=ALU.mult, op1=ALU.add,
-                    )
-                else:
-                    nc.scalar.activation(
-                        out=planes[g][:, t4, :], in_=src, func=ACT.Identity,
-                        scale=wb[:, t4, g : g + 1], bias=wb[:, t4, 2 + g : 3 + g],
-                    )
-                if t == 3 and between is not None:
-                    between()
-                if t == 5:
-                    gx[0] = x_regroup(planes[0])
-            gx[1] = x_regroup(planes[1])
-            x_quantise(q, 0, gx[0])
-            x_quantise(q, 1, gx[1])
-
-        def project(c, q, engines):
-            accs = []
+        def x_transpose(q, g, t):
+            x_bank[q, g, t] = bank()
             for jq in range(4):
-                acc = bank()
+                nc.tensor.transpose(x_bank[q, g, t][:, jq, :], xh[4 * q + jq][:, 4 * g + t, :], perm[:])
+
+        def x_evacuate(q, g, t, eng):
+            if (q, g) not in planes:
+                planes[q, g] = pl_pool.tile([P, 4, 512], BF16, name="planes_t", tag="pl")
+            dst = planes[q, g][:, t, :]
+            src = x_bank[q, g, t][:].rearrange("p a b -> p (a b)")
+            gain, shift = wb[:, t, g : g + 1], wb[:, t, 2 + g : 3 + g]
+            if eng == "v":
+                nc.vector.tensor_scalar(out=dst, in0=src, scalar1=gain, scalar2=shift, op0=ALU.mult, op1=ALU.add)
+            else:
+                nc.scalar.activation(out=dst, in_=src, func=ACT.Identity, scale=gain, bias=shift)
+
+        def x_regroup(q, g):
+            gx[q, g] = gx_pool.tile([P, 512, 4], BF16, name="gx_t", tag="gx", align_bytes=64)
+            nc.vector.tensor_copy(
+                out=gx[q, g][:].rearrange("p (c i) t -> p c t i", i=4),
+                in_=planes[q, g][:].rearrange("p t (c i) -> p c t i", i=4),
+            )
+
+        def x_quantise(q, g):
+            sl = slice((2 * q + g) * 512, (2 * q + g) * 512 + 512)
+            nc.vector.quantize_mx(
+                out=xc[:, sl].bitcast(FP8X4), scales=xs[:, sl], in_=gx[q, g][:].rearrange("p n t -> p (n t)")
+            )
+
+        def multiply(c, q, half):
+            acc = bank()
+            p_bank[c, q, half] = acc
+            for jl in range(2):
                 for g in range(2):
-                    xo = (2 * q + g) * 512 + P * jq
-                    wo = c * 1024 + 512 * g
+                    xo = (2 * q + g) * 512 + P * (2 * half + jl)
+                    wo = c * 512 + 256 * g
                     nc.tensor.matmul_mx(
-                        out=acc[:].rearrange("p a b -> p (a b)"),
+                        out=acc[:, 2 * jl : 2 * jl + 2, :].rearrange("p a b -> p (a b)"),
                         lhsT=xc[:, xo : xo + P].bitcast(FP8X4), lhsT_scale=xs[:, xo : xo + P],
-                        rhs=wc[:, wo : wo + 512].bitcast(FP8X4), rhs_scale=ws[:, wo : wo + 512],
+                        rhs=wc[:, wo : wo + 256].bitcast(FP8X4), rhs_scale=ws[:, wo : wo + 256],
                         start=(g == 0), stop=(g == 1),
                     )
-                accs.append(acc)
-            o_t = o_pool.tile([P, 8, 4, 64], F32, name="o_t", tag="o")
-            for jq in range(4):
-                copy_on(engines[jq], o_t[:, :, jq, :], accs[jq][:].rearrange("p a (x d) -> p (a x) d", d=64))
-            h0 = 8 * (c % 2)
+
+        def out_evacuate(c, q, half, eng):
+            if c not in o_sb:
+                o_sb[c] = o_pool.tile([P, 4, 8, 64], F32, name="o_t", tag="o")
+            j0 = 4 * q + 2 * half
+            copy_on(
+                eng,
+                o_sb[c][:, :, j0 : j0 + 2, :].rearrange("p h j d -> p j h d"),
+                p_bank[c, q, half][:].rearrange("p (j a) (x d) -> p j (a x) d", j=2, d=64),
+            )
+
+        def project(c, q, engines):
+            for half in range(2):
+                multiply(c, q, half)
+                out_evacuate(c, q, half, engines[half])
+
+        def store(c, j0, j1):
+            h0 = 4 * (c % 4)
             for b in range(B):
                 nc.sync.dma_start(
-                    out=outs[c // 2][b, h0 : h0 + 8, :, :].rearrange("h (pp j) d -> pp h j d", j=TILES)[:, :, 4 * q : 4 * q + 4, :],
-                    in_=o_t[b:P:4, :, :, :],
+                    out=outs[c // 4][b, h0 : h0 + 4, :, :].rearrange("h (pp j) d -> pp h j d", j=TILES)[:, :, j0:j1, :],
+                    in_=o_sb[c][b:P:4, :, j0:j1, :],
                 )
 
         nc.vector.memset(lnrow[:], 0.0)
-        nc.scalar.dma_start(out=lnrow[0:2, :], in_=ln_w.rearrange("(r c) -> r c", c=512))
-        nc.scalar.dma_start(out=lnrow[2:4, :], in_=ln_b.rearrange("(r c) -> r c", c=512))
         load_x(0, 1)
         load_x(1, 2)
         load_x(2, 4)
+        load_ln()
         load_w(0)
-        load_x(4, 8)
-        for c in range(1, CHUNKS):
+        load_x(4, 6)
+        load_w(1)
+        load_x(6, 8)
+        for c in range(2, W_BUFS):
             load_w(c)
         make_identity(nc, ident[:])
         nc.vector.memset(one[:], 1.0)
-        nc.scalar.activation(out=warm[:], in_=one[:], func=ACT.Sqrt)
+        nc.scalar.activation(out=warm[:], in_=one[:], func=ACT.Abs_reciprocal_sqrt)
+        nc.vector.tensor_copy(
+            out=perm[:].rearrange("p (pp b) -> p b pp", b=B), in_=ident[:].rearrange("p (b pp) -> p b pp", b=B)
+        )
 
-        for k in range(TILES + 1):
-            if k < TILES:
-                statistics(k)
-            if k >= 1:
-                normalise(k - 1)
-            if k == 1:
-                nc.vector.tensor_copy(out=lnf[:], in_=lnrow[:].rearrange("p (q e) -> p e q", e=4))
-                lnt = bank()
-                for e in range(4):
-                    nc.tensor.transpose(lnt[:, e, :], lnf[:, e, :], ident[:])
-            if k == 2:
-                nc.vector.tensor_copy(out=wb[:], in_=lnt[:, :, 0:4])
-            if k in (3, 4):
-                for r in (2 * (k - 3), 2 * (k - 3) + 1):
-                    w_copy(0, r, w_transposes(0, r), "s")
-
-        prepare_x(0, lambda: w_quantise(0))
-        prepare_w(1, "ssss")
-        prepare_w(2, "ssss")
-        project(0, 0, "sssv")
-        prepare_x(1, None)
-        project(1, 0, "sssv")
-        project(2, 0, "sssv")
-        project(0, 1, "svsv")
-        project(1, 1, "svsv")
-        prepare_w(3, "svsv")
-        project(2, 1, "svsv")
-        prepare_w(4, "svsv")
-        for c in range(3, CHUNKS):
-            project(c, 0, "svsv")
-            if c == 3:
-                prepare_w(5, "svsv")
-            project(c, 1, "svsv")
+        statistics(0)
+        inverse_deviation(0)
+        normalise(0)
+        layer_norm(1)
+        layer_norm(2)
+        ln_rows()
+        w_transpose(0, 0)
+        w_transpose(0, 1)
+        ln_transpose()
+        w_evacuate(0, 0, "s")
+        layer_norm(3)
+        ln_evacuate()
+        w_evacuate(0, 1, "s")
+        layer_norm(4)
+        w_transpose(1, 0)
+        w_transpose(1, 1)
+        w_evacuate(1, 0, "s")
+        layer_norm(5)
+        w_evacuate(1, 1, "s")
+        layer_norm(6)
+        w_prepare(2, "ss")
+        statistics(7)
+        inverse_deviation(7)
+        for g in range(2):
+            for t in range(4):
+                x_transpose(0, g, t)
+        x_evacuate(0, 0, 0, "v")
+        normalise(7, "v")
+        for t, eng in ((1, "s"), (2, "s"), (3, "v")):
+            x_evacuate(0, 0, t, eng)
+        for t in range(4):
+            x_evacuate(0, 1, t, "s")
+        x_regroup(0, 0)
+        x_quantise(0, 0)
+        w_quantise(0)
+        x_regroup(0, 1)
+        x_quantise(0, 1)
+        for g in range(2):
+            for t in range(4):
+                x_transpose(1, g, t)
+                x_evacuate(1, g, t, "v" if (g, t) == (1, 0) else "s")
+        x_regroup(1, 0)
+        x_quantise(1, 0)
+        x_regroup(1, 1)
+        x_quantise(1, 1)
+        project(0, 0, "ss")
+        w_prepare(3, "ss")
+        w_prepare(4, "ss")
+        for c in range(6, CHUNKS):
+            if c < 8:
+                w_reorder(c, "g")
+        w_quantise(1)
+        for c in range(CHUNKS):
+            if c > 0:
+                project(c, 0, "sv")
+            if c == CHUNKS - 1:
+                store(c, 0, 4)
+            if c + 2 < CHUNKS:
+                w_quantise(c + 2)
+            project(c, 1, "sv")
+            if c == CHUNKS - 1:
+                store(c, 4, 8)
+            else:
+                store(c, 0, 8)
+            if c in (2, 4, 6):
+                for n in (c + 3, c + 4):
+                    w_prepare(n, "sv")
+                    if n + 2 < CHUNKS and n >= 6:
+                        w_reorder(n + 2, "g")
+            if c == 8:
+                w_prepare(11, "sv")

@@ -21,7 +21,7 @@ TILES = 8
 CHUNKS = 12
 W_BUFS = 8
 SCALAR_TILES = (1,)
-REORDERED = range(6, CHUNKS)
+REORDERED = ()
 
 
 def tile_selfattention_pa_kernel(tc, inputs, ln_w, ln_b, w_qkv, out_0, out_1, out_2):
@@ -312,9 +312,6 @@ def tile_selfattention_pa_kernel(tc, inputs, ln_w, ln_b, w_qkv, out_0, out_1, ou
         project(0, 0, "ss")
         w_prepare(3, "ss")
         w_prepare(4, "ss")
-        for c in range(6, CHUNKS):
-            if c < 8:
-                w_reorder(c, "g")
         w_quantise(1)
         for c in range(CHUNKS):
             if c > 0:
@@ -331,7 +328,5 @@ def tile_selfattention_pa_kernel(tc, inputs, ln_w, ln_b, w_qkv, out_0, out_1, ou
             if c in (2, 4, 6):
                 for n in (c + 3, c + 4):
                     w_prepare(n, "sv")
-                    if n + 2 < CHUNKS and n >= 6:
-                        w_reorder(n + 2, "g")
             if c == 8:
                 w_prepare(11, "sv")

@@ -35,12 +35,11 @@ def tile_selfattention_pa_kernel(tc, inputs, ln_w, ln_b, w_qkv, out_0, out_1, ou
         xh_pool = ctx.enter_context(tc.tile_pool(name="xh", bufs=8))
         pl_pool = ctx.enter_context(tc.tile_pool(name="pl", bufs=4))
         gx_pool = ctx.enter_context(tc.tile_pool(name="gx", bufs=2))
-        o_pool = ctx.enter_context(tc.tile_pool(name="o", bufs=6))
+        o_pool = ctx.enter_context(tc.tile_pool(name="o", bufs=10))
         ps_pool = ctx.enter_context(tc.psum_pool(name="ps", bufs=8))
         ctx.enter_context(tc.manual_schedule())
 
         ident = const.tile([P, P], F32)
-        perm = const.tile([P, P], F32)
         one = const.tile([P, 1], F32)
         warm = const.tile([P, 1], F32)
         lnrow = const.tile([P, 512], BF16)
@@ -68,11 +67,12 @@ def tile_selfattention_pa_kernel(tc, inputs, ln_w, ln_b, w_qkv, out_0, out_1, ou
         def bank():
             return ps_pool.tile([P, 4, P], F32, name="bank", tag="ps")
 
-        x_rows = inputs.flatten_outer_dims().rearrange("(p j) k -> p j k", j=TILES)
-
         def load_x(j0, j1):
             x_t = const.tile([P, j1 - j0, E], BF16, name="x_t%d" % j0)
-            nc.sync.dma_start(out=x_t[:], in_=x_rows[:, j0:j1, :])
+            b = j0 // 2
+            nc.sync.dma_start(
+                out=x_t[:], in_=inputs[b].rearrange("(p j) k -> p j k", j=2)[:, j0 - 2 * b : j1 - 2 * b, :]
+            )
             for j in range(j0, j1):
                 x_sb[j] = x_t[:, j - j0, :]
 
@@ -183,7 +183,7 @@ def tile_selfattention_pa_kernel(tc, inputs, ln_w, ln_b, w_qkv, out_0, out_1, ou
         def x_transpose(q, g, t):
             x_bank[q, g, t] = bank()
             for jq in range(4):
-                nc.tensor.transpose(x_bank[q, g, t][:, jq, :], xh[4 * q + jq][:, 4 * g + t, :], perm[:])
+                nc.tensor.transpose(x_bank[q, g, t][:, jq, :], xh[4 * q + jq][:, 4 * g + t, :], ident[:])
 
         def x_evacuate(q, g, t, eng):
             if (q, g) not in planes:
@@ -224,13 +224,12 @@ def tile_selfattention_pa_kernel(tc, inputs, ln_w, ln_b, w_qkv, out_0, out_1, ou
                     )
 
         def out_evacuate(c, q, half, eng):
-            if c not in o_sb:
-                o_sb[c] = o_pool.tile([P, 4, 8, 64], F32, name="o_t", tag="o")
-            j0 = 4 * q + 2 * half
+            if (c, q) not in o_sb:
+                o_sb[c, q] = o_pool.tile([P, 2, 4, 2, 64], F32, name="o_t", tag="o")
             copy_on(
                 eng,
-                o_sb[c][:, :, j0 : j0 + 2, :].rearrange("p h j d -> p j h d"),
-                p_bank[c, q, half][:].rearrange("p (j a) (x d) -> p j (a x) d", j=2, d=64),
+                o_sb[c, q][:, half, :, :, :],
+                p_bank[c, q, half][:].rearrange("p (j a) (x d) -> p (a x) j d", j=2, d=64),
             )
 
         def project(c, q, engines):
@@ -238,12 +237,12 @@ def tile_selfattention_pa_kernel(tc, inputs, ln_w, ln_b, w_qkv, out_0, out_1, ou
                 multiply(c, q, half)
                 out_evacuate(c, q, half, engines[half])
 
-        def store(c, j0, j1):
+        def store(c, q):
             h0 = 4 * (c % 4)
-            for b in range(B):
+            for half in range(2):
                 nc.sync.dma_start(
-                    out=outs[c // 4][b, h0 : h0 + 4, :, :].rearrange("h (pp j) d -> pp h j d", j=TILES)[:, :, j0:j1, :],
-                    in_=o_sb[c][b:P:4, :, j0:j1, :],
+                    out=outs[c // 4][2 * q + half, h0 : h0 + 4, :, :].rearrange("h (p j) d -> p h (j d)", j=2),
+                    in_=o_sb[c, q][:, half, :, :, :].rearrange("p h j d -> p h (j d)"),
                 )
 
         nc.vector.memset(lnrow[:], 0.0)
@@ -260,9 +259,6 @@ def tile_selfattention_pa_kernel(tc, inputs, ln_w, ln_b, w_qkv, out_0, out_1, ou
         make_identity(nc, ident[:])
         nc.vector.memset(one[:], 1.0)
         nc.scalar.activation(out=warm[:], in_=one[:], func=ACT.Abs_reciprocal_sqrt)
-        nc.vector.tensor_copy(
-            out=perm[:].rearrange("p (pp b) -> p b pp", b=B), in_=ident[:].rearrange("p (b pp) -> p b pp", b=B)
-        )
 
         statistics(0)
         inverse_deviation(0)
@@ -310,21 +306,18 @@ def tile_selfattention_pa_kernel(tc, inputs, ln_w, ln_b, w_qkv, out_0, out_1, ou
         x_regroup(1, 1)
         x_quantise(1, 1)
         project(0, 0, "ss")
+        store(0, 0)
         w_prepare(3, "ss")
         w_prepare(4, "ss")
         w_quantise(1)
         for c in range(CHUNKS):
             if c > 0:
                 project(c, 0, "sv")
-            if c == CHUNKS - 1:
-                store(c, 0, 4)
+                store(c, 0)
             if c + 2 < CHUNKS:
                 w_quantise(c + 2)
             project(c, 1, "sv")
-            if c == CHUNKS - 1:
-                store(c, 4, 8)
-            else:
-                store(c, 0, 8)
+            store(c, 1)
             if c in (2, 4, 6):
                 for n in (c + 3, c + 4):
                     w_prepare(n, "sv")

@@ -318,8 +318,5 @@ def tile_selfattention_pa_kernel(tc, inputs, ln_w, ln_b, w_qkv, out_0, out_1, ou
                 w_quantise(c + 2)
             project(c, 1, "sv")
             store(c, 1)
-            if c in (2, 4, 6):
-                for n in (c + 3, c + 4):
-                    w_prepare(n, "sv")
-            if c == 8:
-                w_prepare(11, "sv")
+            if c + 4 < CHUNKS and c > 0:
+                w_prepare(c + 4, "sv")

@@ -21,7 +21,6 @@ TILES = 8
 CHUNKS = 12
 W_BUFS = 8
 SCALAR_TILES = (1,)
-REORDERED = ()
 
 
 def tile_selfattention_pa_kernel(tc, inputs, ln_w, ln_b, w_qkv, out_0, out_1, out_2):
@@ -30,7 +29,6 @@ def tile_selfattention_pa_kernel(tc, inputs, ln_w, ln_b, w_qkv, out_0, out_1, ou
     with ExitStack() as ctx:
         const = ctx.enter_context(tc.tile_pool(name="const", bufs=1))
         wraw_pool = ctx.enter_context(tc.tile_pool(name="wraw", bufs=W_BUFS))
-        wp_pool = ctx.enter_context(tc.tile_pool(name="wp", bufs=2))
         gw_pool = ctx.enter_context(tc.tile_pool(name="gw", bufs=6))
         xh_pool = ctx.enter_context(tc.tile_pool(name="xh", bufs=8))
         pl_pool = ctx.enter_context(tc.tile_pool(name="pl", bufs=4))
@@ -88,16 +86,22 @@ def tile_selfattention_pa_kernel(tc, inputs, ln_w, ln_b, w_qkv, out_0, out_1, ou
             )
             wraw[c] = w_t
 
-        def statistics(j):
-            if j in SCALAR_TILES:
-                nc.scalar.activation(out=junk[:], in_=x_sb[j], func=ACT.Identity, accum_out=sums[:, j, 0:1])
-                nc.scalar.activation(out=negmu[:, j : j + 1], in_=sums[:, j, 0:1], func=ACT.Identity, scale=-1.0 / E)
-                nc.scalar.activation(
-                    out=junk[:], in_=x_sb[j], func=ACT.Square, bias=negmu[:, j : j + 1], accum_out=sums[:, j, 1:2]
-                )
-                return
+        def sum_on_scalar(j):
+            nc.scalar.activation(out=junk[:], in_=x_sb[j], func=ACT.Identity, accum_out=sums[:, j, 0:1])
+
+        def squares_on_scalar(j):
+            nc.scalar.activation(out=negmu[:, j : j + 1], in_=sums[:, j, 0:1], func=ACT.Identity, scale=-1.0 / E)
+            nc.scalar.activation(
+                out=junk[:], in_=x_sb[j], func=ACT.Square, bias=negmu[:, j : j + 1], accum_out=sums[:, j, 1:2]
+            )
+
+        def statistics(j, between=None):
             for h in range(2):
                 nc.vector.bn_stats(out=st[:, j, h, :], in_=x_sb[j][:, 512 * h : 512 * h + 512])
+                if h == 0 and between is not None:
+                    aggregate(between)
+
+        def aggregate(j):
             nc.vector.bn_aggr(out=mv[:, j, :], in_=st[:, j, :, :].rearrange("p a b -> p (a b)"))
 
         def inverse_deviation(j):
@@ -107,6 +111,7 @@ def tile_selfattention_pa_kernel(tc, inputs, ln_w, ln_b, w_qkv, out_0, out_1, ou
                 )
             else:
                 nc.scalar.activation(out=rstd[:, j : j + 1], in_=mv[:, j, 1:2], func=ACT.Abs_reciprocal_sqrt, bias=EPS)
+                nc.scalar.activation(out=negmu[:, j : j + 1], in_=mv[:, j, 0:1], func=ACT.Identity, scale=-1.0)
 
         def normalise(j, eng="g"):
             xh[j] = xh_pool.tile([P, 8, P], F32, name="xh_t", tag="xh")
@@ -117,16 +122,11 @@ def tile_selfattention_pa_kernel(tc, inputs, ln_w, ln_b, w_qkv, out_0, out_1, ou
                     out=dst, in0=src, scalar1=mv[:, j, 0:1], scalar2=rstd[:, j : j + 1], op0=ALU.subtract, op1=ALU.mult
                 )
                 return
-            if j not in SCALAR_TILES:
-                nc.gpsimd.tensor_scalar(
-                    out=negmu[:, j : j + 1], in0=mv[:, j, 0:1], scalar1=-1.0, scalar2=0.0, op0=ALU.mult, op1=ALU.add
-                )
             nc.gpsimd.tensor_scalar(
                 out=dst, in0=src, scalar1=negmu[:, j : j + 1], scalar2=rstd[:, j : j + 1], op0=ALU.add, op1=ALU.mult
             )
 
-        def layer_norm(j, eng="g"):
-            statistics(j)
+        def scale(j, eng="g"):
             inverse_deviation(j)
             normalise(j, eng)
 
@@ -141,27 +141,13 @@ def tile_selfattention_pa_kernel(tc, inputs, ln_w, ln_b, w_qkv, out_0, out_1, ou
         def ln_evacuate():
             nc.scalar.copy(out=wb[:], in_=ln_bank[0][:, :, 0:4])
 
-        def w_reorder(c, eng):
-            wp[c] = wp_pool.tile([P, 2 * E], BF16, name="wp_t", tag="wp")
-            for u in range(2):
-                dst = wp[c][:].rearrange("p (rg u q e) -> p u rg q e", rg=4, u=2, e=2)[:, u, :, :, :]
-                src = wraw[c][:].rearrange("p (rg q u e) -> p u rg q e", rg=4, u=2, e=2)[:, u, :, :, :]
-                if eng == "g":
-                    nc.gpsimd.tensor_scalar(out=dst, in0=src, scalar1=1.0, scalar2=0.0, op0=ALU.mult, op1=ALU.add)
-                else:
-                    nc.vector.tensor_copy(out=dst, in_=src)
-
         def w_transpose(c, g):
             w_bank[c, g] = bank()
-            words = (wp[c] if c in REORDERED else wraw[c])[:].bitcast(F32)
+            words = wraw[c][:].bitcast(F32)
             for r in range(2):
                 for u in range(2):
-                    first = 512 * r + 256 * g
-                    if c in REORDERED:
-                        w128 = words[:, first + P * u : first + P * u + P]
-                    else:
-                        w128 = words[:, first + u : first + u + 255 : 2]
-                    nc.tensor.transpose(w_bank[c, g][:, 2 * r + u, :], w128, ident[:])
+                    first = 512 * r + 256 * g + u
+                    nc.tensor.transpose(w_bank[c, g][:, 2 * r + u, :], words[:, first : first + 255 : 2], ident[:])
             if g == 1 and c + W_BUFS < CHUNKS:
                 load_w(c + W_BUFS)
 
@@ -260,10 +246,17 @@ def tile_selfattention_pa_kernel(tc, inputs, ln_w, ln_b, w_qkv, out_0, out_1, ou
         nc.vector.memset(one[:], 1.0)
         nc.scalar.activation(out=warm[:], in_=one[:], func=ACT.Abs_reciprocal_sqrt)
 
+        def layer_norm(j):
+            statistics(j)
+            aggregate(j)
+            scale(j)
+
         statistics(0)
-        inverse_deviation(0)
-        normalise(0)
-        layer_norm(1)
+        aggregate(0)
+        scale(0)
+        sum_on_scalar(1)
+        squares_on_scalar(1)
+        scale(1)
         layer_norm(2)
         ln_rows()
         w_transpose(0, 0)
@@ -282,6 +275,7 @@ def tile_selfattention_pa_kernel(tc, inputs, ln_w, ln_b, w_qkv, out_0, out_1, ou
         layer_norm(6)
         w_prepare(2, "ss")
         statistics(7)
+        aggregate(7)
         inverse_deviation(7)
         for g in range(2):
             for t in range(4):

from contextlib import ExitStack

import concourse.mybir as mybir
from concourse.masks import make_identity

FLOPS = 2 * 1024 * 3072 * 1024

F32 = mybir.dt.float32
BF16 = mybir.dt.bfloat16
U32 = mybir.dt.uint32
U8 = mybir.dt.uint8
FP8X4 = mybir.dt.float8_e4m3fn_x4
ALU = mybir.AluOpType
ACT = mybir.ActivationFunctionType

P = 128
B = 4
E = 1024
EPS = 1e-5
TILES = 8
CHUNKS = 12
W_BUFS = 8
SCALAR_TILES = (1,)


def tile_selfattention_pa_kernel(tc, inputs, ln_w, ln_b, w_qkv, out_0, out_1, out_2):
    nc = tc.nc
    outs = (out_0, out_1, out_2)
    with ExitStack() as ctx:
        const = ctx.enter_context(tc.tile_pool(name="const", bufs=1))
        wraw_pool = ctx.enter_context(tc.tile_pool(name="wraw", bufs=W_BUFS))
        gw_pool = ctx.enter_context(tc.tile_pool(name="gw", bufs=6))
        xh_pool = ctx.enter_context(tc.tile_pool(name="xh", bufs=8))
        pl_pool = ctx.enter_context(tc.tile_pool(name="pl", bufs=4))
        gx_pool = ctx.enter_context(tc.tile_pool(name="gx", bufs=2))
        o_pool = ctx.enter_context(tc.tile_pool(name="o", bufs=10))
        ps_pool = ctx.enter_context(tc.psum_pool(name="ps", bufs=8))
        ctx.enter_context(tc.manual_schedule())

        ident = const.tile([P, P], F32)
        one = const.tile([P, 1], F32)
        warm = const.tile([P, 1], F32)
        lnrow = const.tile([P, 512], BF16)
        lnf = const.tile([P, 4, P], F32)
        wb = const.tile([P, 4, 4], F32)
        xc = const.tile([P, 2 * 2 * 512], U32, align_bytes=64)
        xs = const.tile([P, 2 * 2 * 512], U8, align_bytes=64)
        wc = const.tile([P, CHUNKS * 512], U32, align_bytes=64)
        ws = const.tile([P, CHUNKS * 512], U8, align_bytes=64)
        st = const.tile([P, TILES, 2, 6], F32)
        mv = const.tile([P, TILES, 2], F32)
        rstd = const.tile([P, TILES], F32)
        negmu = const.tile([P, TILES], F32)
        junk = const.tile([P, E], BF16)
        sums = const.tile([P, TILES, 2], F32)
        x_sb, xh, wraw, gw, wp, o_sb, planes, gx = {}, {}, {}, {}, {}, {}, {}, {}
        w_bank, x_bank, p_bank, ln_bank = {}, {}, {}, {}

        def copy_on(eng, dst, src):
            if eng == "v":
                nc.vector.tensor_copy(out=dst, in_=src)
            else:
                nc.scalar.copy(out=dst, in_=src)

        def bank():
            return ps_pool.tile([P, 4, P], F32, name="bank", tag="ps")

        def load_x(j0, j1):
            x_t = const.tile([P, j1 - j0, E], BF16, name="x_t%d" % j0)
            b = j0 // 2
            nc.sync.dma_start(
                out=x_t[:], in_=inputs[b].rearrange("(p j) k -> p j k", j=2)[:, j0 - 2 * b : j1 - 2 * b, :]
            )
            for j in range(j0, j1):
                x_sb[j] = x_t[:, j - j0, :]

        def load_ln():
            nc.sync.dma_start(out=lnrow[0:2, :], in_=ln_w.rearrange("(r c) -> r c", c=512))
            nc.sync.dma_start(out=lnrow[2:4, :], in_=ln_b.rearrange("(r c) -> r c", c=512))

        def load_w(c):
            w_t = wraw_pool.tile([P, 2 * E], BF16, name="wraw_t", tag="wraw")
            nc.sync.dma_start(
                out=w_t[:].rearrange("p (r k) -> p r k", r=2),
                in_=w_qkv[256 * c : 256 * c + 256, :].rearrange("(r p) k -> p r k", p=P),
            )
            wraw[c] = w_t

        def sum_on_scalar(j):
            nc.scalar.activation(out=junk[:], in_=x_sb[j], func=ACT.Identity, accum_out=sums[:, j, 0:1])

        def squares_on_scalar(j):
            nc.scalar.activation(out=negmu[:, j : j + 1], in_=sums[:, j, 0:1], func=ACT.Identity, scale=-1.0 / E)
            nc.scalar.activation(
                out=junk[:], in_=x_sb[j], func=ACT.Square, bias=negmu[:, j : j + 1], accum_out=sums[:, j, 1:2]
            )

        def statistics(j, between=None):
            for h in range(2):
                nc.vector.bn_stats(out=st[:, j, h, :], in_=x_sb[j][:, 512 * h : 512 * h + 512])
                if h == 0 and between is not None:
                    aggregate(between)

        def aggregate(j):
            nc.vector.bn_aggr(out=mv[:, j, :], in_=st[:, j, :, :].rearrange("p a b -> p (a b)"))

        def inverse_deviation(j):
            if j in SCALAR_TILES:
                nc.scalar.activation(
                    out=rstd[:, j : j + 1], in_=sums[:, j, 1:2], func=ACT.Abs_reciprocal_sqrt, bias=EPS, scale=1.0 / E
                )
            else:
                nc.scalar.activation(out=rstd[:, j : j + 1], in_=mv[:, j, 1:2], func=ACT.Abs_reciprocal_sqrt, bias=EPS)
                nc.scalar.activation(out=negmu[:, j : j + 1], in_=mv[:, j, 0:1], func=ACT.Identity, scale=-1.0)

        def normalise(j, eng="g"):
            xh[j] = xh_pool.tile([P, 8, P], F32, name="xh_t", tag="xh")
            dst = xh[j][:].rearrange("p (g t) q -> p g t q", t=4)
            src = x_sb[j].rearrange("p (g q t) -> p g t q", g=2, t=4)
            if eng == "v":
                nc.vector.tensor_scalar(
                    out=dst, in0=src, scalar1=mv[:, j, 0:1], scalar2=rstd[:, j : j + 1], op0=ALU.subtract, op1=ALU.mult
                )
                return
            nc.gpsimd.tensor_scalar(
                out=dst, in0=src, scalar1=negmu[:, j : j + 1], scalar2=rstd[:, j : j + 1], op0=ALU.add, op1=ALU.mult
            )

        def scale(j, eng="g"):
            inverse_deviation(j)
            normalise(j, eng)

        def ln_rows():
            nc.scalar.copy(out=lnf[:], in_=lnrow[:].rearrange("p (q e) -> p e q", e=4))

        def ln_transpose():
            ln_bank[0] = bank()
            for t in range(4):
                nc.tensor.transpose(ln_bank[0][:, t, :], lnf[:, t, :], ident[:])

        def ln_evacuate():
            nc.scalar.copy(out=wb[:], in_=ln_bank[0][:, :, 0:4])

        def w_transpose(c, g):
            w_bank[c, g] = bank()
            words = wraw[c][:].bitcast(F32)
            for r in range(2):
                for u in range(2):
                    first = 512 * r + 256 * g + u
                    nc.tensor.transpose(w_bank[c, g][:, 2 * r + u, :], words[:, first : first + 255 : 2], ident[:])
            if g == 1 and c + W_BUFS < CHUNKS:
                load_w(c + W_BUFS)

        def w_evacuate(c, g, eng):
            if c not in gw:
                gw[c] = gw_pool.tile([P, 2048], BF16, name="gw_t", tag="gw", align_bytes=64)
            dst = gw[c][:].bitcast(F32).rearrange("p (g r n u) -> p g r n u", g=2, r=2, u=2)[:, g, :, :, :]
            copy_on(eng, dst, w_bank[c, g][:].rearrange("p (r u) n -> p r n u", u=2))

        def w_prepare(c, engines):
            for g in range(2):
                w_transpose(c, g)
                w_evacuate(c, g, engines[g])

        def w_quantise(c):
            sl = slice(c * 512, c * 512 + 512)
            nc.vector.quantize_mx(out=wc[:, sl].bitcast(FP8X4), scales=ws[:, sl], in_=gw[c][:])

        def x_transpose(q, g, t):
            x_bank[q, g, t] = bank()
            for jq in range(4):
                nc.tensor.transpose(x_bank[q, g, t][:, jq, :], xh[4 * q + jq][:, 4 * g + t, :], ident[:])

        def x_evacuate(q, g, t, eng):
            if (q, g) not in planes:
                planes[q, g] = pl_pool.tile([P, 4, 512], BF16, name="planes_t", tag="pl")
            dst = planes[q, g][:, t, :]
            src = x_bank[q, g, t][:].rearrange("p a b -> p (a b)")
            gain, shift = wb[:, t, g : g + 1], wb[:, t, 2 + g : 3 + g]
            if eng == "v":
                nc.vector.tensor_scalar(out=dst, in0=src, scalar1=gain, scalar2=shift, op0=ALU.mult, op1=ALU.add)
            else:
                nc.scalar.activation(out=dst, in_=src, func=ACT.Identity, scale=gain, bias=shift)

        def x_regroup(q, g):
            gx[q, g] = gx_pool.tile([P, 512, 4], BF16, name="gx_t", tag="gx", align_bytes=64)
            nc.vector.tensor_copy(
                out=gx[q, g][:].rearrange("p (c i) t -> p c t i", i=4),
                in_=planes[q, g][:].rearrange("p t (c i) -> p c t i", i=4),
            )

        def x_quantise(q, g):
            sl = slice((2 * q + g) * 512, (2 * q + g) * 512 + 512)
            nc.vector.quantize_mx(
                out=xc[:, sl].bitcast(FP8X4), scales=xs[:, sl], in_=gx[q, g][:].rearrange("p n t -> p (n t)")
            )

        def multiply(c, q, half):
            acc = bank()
            p_bank[c, q, half] = acc
            for jl in range(2):
                for g in range(2):
                    xo = (2 * q + g) * 512 + P * (2 * half + jl)
                    wo = c * 512 + 256 * g
                    nc.tensor.matmul_mx(
                        out=acc[:, 2 * jl : 2 * jl + 2, :].rearrange("p a b -> p (a b)"),
                        lhsT=xc[:, xo : xo + P].bitcast(FP8X4), lhsT_scale=xs[:, xo : xo + P],
                        rhs=wc[:, wo : wo + 256].bitcast(FP8X4), rhs_scale=ws[:, wo : wo + 256],
                        start=(g == 0), stop=(g == 1),
                    )

        def out_evacuate(c, q, half, eng):
            if (c, q) not in o_sb:
                o_sb[c, q] = o_pool.tile([P, 2, 4, 2, 64], F32, name="o_t", tag="o")
            copy_on(
                eng,
                o_sb[c, q][:, half, :, :, :],
                p_bank[c, q, half][:].rearrange("p (j a) (x d) -> p (a x) j d", j=2, d=64),
            )

        def project(c, q, engines):
            for half in range(2):
                multiply(c, q, half)
                out_evacuate(c, q, half, engines[half])

        def store(c, q):
            h0 = 4 * (c % 4)
            for half in range(2):
                nc.sync.dma_start(
                    out=outs[c // 4][2 * q + half, h0 : h0 + 4, :, :].rearrange("h (p j) d -> p h (j d)", j=2),
                    in_=o_sb[c, q][:, half, :, :, :].rearrange("p h j d -> p h (j d)"),
                )

        nc.vector.memset(lnrow[:], 0.0)
        load_x(0, 1)
        load_x(1, 2)
        load_x(2, 4)
        load_ln()
        load_w(0)
        load_x(4, 6)
        load_w(1)
        load_x(6, 8)
        for c in range(2, W_BUFS):
            load_w(c)
        make_identity(nc, ident[:])
        nc.vector.memset(one[:], 1.0)
        nc.scalar.activation(out=warm[:], in_=one[:], func=ACT.Abs_reciprocal_sqrt)

        def layer_norm(j):
            statistics(j)
            aggregate(j)
            scale(j)

        statistics(0)
        aggregate(0)
        scale(0)
        sum_on_scalar(1)
        squares_on_scalar(1)
        scale(1)
        layer_norm(2)
        ln_rows()
        w_transpose(0, 0)
        w_transpose(0, 1)
        ln_transpose()
        w_evacuate(0, 0, "s")
        layer_norm(3)
        ln_evacuate()
        w_evacuate(0, 1, "s")
        layer_norm(4)
        w_transpose(1, 0)
        w_transpose(1, 1)
        w_evacuate(1, 0, "s")
        layer_norm(5)
        w_evacuate(1, 1, "s")
        layer_norm(6)
        w_prepare(2, "ss")
        statistics(7)
        aggregate(7)
        inverse_deviation(7)
        for g in range(2):
            for t in range(4):
                x_transpose(0, g, t)
        x_evacuate(0, 0, 0, "v")
        normalise(7, "v")
        for t, eng in ((1, "s"), (2, "s"), (3, "v")):
            x_evacuate(0, 0, t, eng)
        for t in range(4):
            x_evacuate(0, 1, t, "s")
        x_regroup(0, 0)
        x_quantise(0, 0)
        w_quantise(0)
        x_regroup(0, 1)
        x_quantise(0, 1)
        for g in range(2):
            for t in range(4):
                x_transpose(1, g, t)
                x_evacuate(1, g, t, "v" if (g, t) == (1, 0) else "s")
        x_regroup(1, 0)
        x_quantise(1, 0)
        x_regroup(1, 1)
        x_quantise(1, 1)
        project(0, 0, "ss")
        store(0, 0)
        w_prepare(3, "ss")
        w_prepare(4, "ss")
        w_quantise(1)
        for c in range(CHUNKS):
            if c > 0:
                project(c, 0, "sv")
                store(c, 0)
            if c + 2 < CHUNKS:
                w_quantise(c + 2)
            project(c, 1, "sv")
            store(c, 1)
            if c + 4 < CHUNKS and c > 0:
                w_prepare(c + 4, "sv")
